import numpy as np
import ml_dtypes


def mxq(x, axis, fmt="e4m3"):
    dtype, down = {"e4m3": (ml_dtypes.float8_e4m3fn, 7), "e5m2": (ml_dtypes.float8_e5m2, 14)}[fmt]
    v = np.moveaxis(np.asarray(x, np.float32).astype(ml_dtypes.bfloat16).astype(np.float64), axis, -1)
    blocks = v.reshape(v.shape[:-1] + (-1, 32))
    amax = np.abs(blocks).max(-1, keepdims=True)
    byte = np.maximum(np.where(amax > 0, np.frexp(amax)[1] - 1 + 127, 0) - down, 1)
    scale = np.exp2(byte - 127.0)
    codes = (blocks / scale).astype(np.float32).astype(dtype).astype(np.float64)
    return np.moveaxis((codes * scale).reshape(v.shape), -1, axis)


WIDE = False


def mx_kscale(k):
    if not WIDE:
        return np.ones(k)
    levels = np.array([10, -10, 5, -5, 0])
    a = np.random.permutation(np.resize(levels, k // 512 * 4)).reshape(k // 512, 4)
    idx = np.arange(k)
    return np.exp2(a[idx // 512, idx % 128 // 32])


BF16 = ml_dtypes.bfloat16


def bf(x):
    return np.asarray(x, np.float32).astype(BF16)


def f64(x):
    return np.asarray(x).astype(np.float64)


ND, NS, D0, D1, D2, D3, DH, C = 640, 16384, 512, 128, 256, 512, 256, 10
SIG = 4.0


def draw_adj():
    w = np.exp(SIG * np.random.standard_normal((ND, NS)))
    return w / w.sum(1, keepdims=True)


def setup_inputs():
    s = mx_kscale(D0)
    return {"x": bf(np.random.standard_normal((NS, D0)) * s),
            "adj": bf(draw_adj()),
            "W0": bf(np.random.standard_normal((D0, D1)) * 2.0 / np.sqrt(D0) / s[:, None]),
            "b0": bf(np.random.standard_normal(D1) * 0.5)}


def reference(x, adj, W0, b0):
    h = (mxq(f64(x), 1, "e4m3") @ mxq(f64(W0), 0, "e4m3")) + f64(b0)
    return np.maximum(mxq(f64(adj), 1, "e4m3") @ mxq(h, 0, "e4m3"), 0.0)

@@ -1,0 +1,203 @@
+import concourse.mybir as mybir
+from concourse.masks import make_identity
+
+F32 = mybir.dt.float32
+BF16 = mybir.dt.bfloat16
+U32 = mybir.dt.uint32
+U8 = mybir.dt.uint8
+FP8X4 = mybir.dt.float8_e4m3fn_x4
+
+N_DST, N_SRC, D_IN, D_OUT = 640, 16384, 512, 128
+FLOPS = 2 * N_SRC * D_IN * D_OUT + 2 * N_DST * N_SRC * D_OUT
+
+P = 128
+PACK = 4
+K_PASS = P * PACK
+CHUNK = 4096
+BANK_WORDS = 512
+BLOCKS_PER_BANK = BANK_WORDS // P
+BANKS = CHUNK // 2 // BANK_WORDS
+OPERANDS = CHUNK // K_PASS
+
+X_NODES = CHUNK // D_IN * P
+X_ROUNDS = N_SRC // X_NODES
+H_PASSES = OPERANDS // PACK
+ADJ_CHUNKS = N_SRC // CHUNK
+ADJ_ROUNDS = N_DST // P * ADJ_CHUNKS
+ROUNDS = X_ROUNDS + ADJ_ROUNDS
+
+VECTOR_BANKS_X = 0
+VECTOR_BANKS_ADJ = 1
+
+CHUNK_BUFS = 16
+XPOSE_BANKS = 6
+
+
+def tile_gcn_pa_k_kernel(tc, x, adj, W0, b0, out):
+    nc = tc.nc
+    with (
+        tc.tile_pool(name="const", bufs=1) as const,
+        tc.tile_pool(name="stream", bufs=CHUNK_BUFS) as stream,
+        tc.tile_pool(name="work", bufs=3) as work,
+        tc.psum_pool(name="xpose", bufs=XPOSE_BANKS) as xpose,
+        tc.psum_pool(name="sums", bufs=2) as sums,
+        tc.manual_schedule(),
+    ):
+        chunks = []
+        for r in range(ROUNDS):
+            chunk = stream.tile([P, CHUNK], BF16, name="chunk")
+            if r < X_ROUNDS:
+                nodes = x[r * X_NODES : (r + 1) * X_NODES, :]
+                nc.sync.dma_start(
+                    out=chunk[:].rearrange("p (b w) -> p b w", w=2 * D_IN),
+                    in_=nodes.rearrange("(b p e) f -> p b (e f)", p=P, e=2),
+                )
+            else:
+                a, c = divmod(r - X_ROUNDS, ADJ_CHUNKS)
+                nc.sync.dma_start(
+                    out=chunk[:], in_=adj[a * P : (a + 1) * P, c * CHUNK : (c + 1) * CHUNK]
+                )
+            chunks.append(chunk)
+
+        ones = const.tile([P, P], BF16, name="ones")
+        nc.vector.memset(ones[:], 1.0)
+        b_rows = const.tile([P, D_OUT], BF16, name="b_rows")
+        nc.vector.memset(b_rows[:], 0.0)
+        nc.scalar.dma_start(out=b_rows[0:1, :], in_=b0.unsqueeze(0))
+        b_sum = sums.tile([P, D_OUT], F32, name="mx_sum")
+        nc.tensor.matmul(out=b_sum[:], lhsT=ones[:], rhs=b_rows[:], start=True, stop=True)
+        bias = const.tile([P, D_OUT], F32, name="bias")
+        nc.vector.tensor_copy(out=bias[:], in_=b_sum[:])
+
+        w_raw = const.tile([P, PACK, D_OUT], BF16, name="w_raw")
+        nc.scalar.dma_start(
+            out=w_raw[:].rearrange("p (u e) c -> p u (e c)", e=2),
+            in_=W0.rearrange("(u p e) c -> p u (e c)", p=P, e=2),
+        )
+        w_grouped = const.tile([P, D_OUT, PACK], BF16, name="w_grouped", align_bytes=64)
+        nc.vector.tensor_copy(out=w_grouped[:], in_=w_raw[:].rearrange("p t c -> p c t"))
+        w_codes = const.tile([P, D_OUT], U32, name="w_codes", align_bytes=64)
+        w_scales = const.tile([P, D_OUT], U8, name="w_scales", align_bytes=64)
+        nc.vector.quantize_mx(
+            out=w_codes[:].bitcast(FP8X4),
+            scales=w_scales[:],
+            in_=w_grouped[:].rearrange("p c t -> p (c t)"),
+        )
+
+        ident = const.tile([P, P], F32, name="ident")
+        make_identity(nc, ident[:])
+
+        h_codes = const.tile([P, N_SRC // K_PASS * D_OUT], U32, name="h_codes", align_bytes=64)
+        h_scales = const.tile([P, N_SRC // K_PASS * D_OUT], U8, name="h_scales", align_bytes=64)
+
+        grouped_of = {}
+        codes_of = {}
+        scales_of = {}
+        sums_of = {}
+        h_grouped_of = {}
+
+        def transpose(r):
+            words = chunks[r][:].bitcast(F32)
+            grouped = work.tile([P, CHUNK], BF16, name="grouped", align_bytes=64)
+            grouped_words = grouped[:].bitcast(F32)
+            vector_banks = VECTOR_BANKS_X if r < X_ROUNDS else VECTOR_BANKS_ADJ
+            for k in range(BANKS):
+                bank = xpose.tile([P, BANK_WORDS], F32, name="bank")
+                for j in range(BLOCKS_PER_BANK):
+                    block = k * BLOCKS_PER_BANK + j
+                    nc.tensor.transpose(
+                        bank[:, j * P : (j + 1) * P], words[:, block * P : (block + 1) * P], ident[:]
+                    )
+                src = bank[:].rearrange("p (m u c) -> p m c u", u=2, c=P)
+                dst = grouped_words[:, k * BANK_WORDS : (k + 1) * BANK_WORDS].rearrange(
+                    "p (m c u) -> p m c u", u=2, c=P
+                )
+                if k < BANKS - vector_banks:
+                    nc.scalar.copy(out=dst, in_=src)
+                else:
+                    nc.vector.tensor_copy(out=dst, in_=src)
+            grouped_of[r] = grouped
+
+        def quantise(r):
+            codes = work.tile([P, OPERANDS * P], U32, name="codes", align_bytes=64)
+            scales = work.tile([P, OPERANDS * P], U8, name="scales", align_bytes=64)
+            nc.vector.quantize_mx(
+                out=codes[:].bitcast(FP8X4), scales=scales[:], in_=grouped_of[r][:]
+            )
+            codes_of[r] = codes
+            scales_of[r] = scales
+
+        def multiply(r):
+            codes = codes_of[r]
+            scales = scales_of[r]
+            if r < X_ROUNDS:
+                sums_of[r] = []
+                for g in range(H_PASSES):
+                    h_sum = sums.tile([P, PACK, D_OUT], F32, name="mx_sum")
+                    for t in range(PACK):
+                        cols = slice((g * PACK + t) * P, (g * PACK + t + 1) * P)
+                        nc.tensor.matmul_mx(
+                            out=h_sum[:, t, :],
+                            lhsT=codes[:, cols].bitcast(FP8X4),
+                            lhsT_scale=scales[:, cols],
+                            rhs=w_codes[:].bitcast(FP8X4),
+                            rhs_scale=w_scales[:],
+                            start=True,
+                            stop=True,
+                        )
+                    sums_of[r].append(h_sum)
+            else:
+                c = (r - X_ROUNDS) % ADJ_CHUNKS
+                if c == 0:
+                    out_sum = sums.tile([P, D_OUT], F32, name="mx_sum")
+                else:
+                    out_sum = sums_of[r - 1]
+                for m in range(OPERANDS):
+                    g = c * OPERANDS + m
+                    nc.tensor.matmul_mx(
+                        out=out_sum[:],
+                        lhsT=codes[:, m * P : (m + 1) * P].bitcast(FP8X4),
+                        lhsT_scale=scales[:, m * P : (m + 1) * P],
+                        rhs=h_codes[:, g * D_OUT : (g + 1) * D_OUT].bitcast(FP8X4),
+                        rhs_scale=h_scales[:, g * D_OUT : (g + 1) * D_OUT],
+                        start=(g == 0),
+                        stop=(g == N_SRC // K_PASS - 1),
+                    )
+                sums_of[r] = out_sum
+
+        def finish(r):
+            if r < X_ROUNDS:
+                h_grouped = work.tile([P, H_PASSES, D_OUT, PACK], BF16, name="h_grouped", align_bytes=64)
+                for g, h_sum in enumerate(sums_of[r]):
+                    nc.vector.tensor_tensor(
+                        out=h_grouped[:, g, :, :],
+                        in0=h_sum[:].rearrange("p t d -> p d t"),
+                        in1=bias[:].unsqueeze(2).to_broadcast([P, D_OUT, PACK]),
+                        op=mybir.AluOpType.add,
+                    )
+                h_grouped_of[r] = h_grouped
+            elif (r - X_ROUNDS) % ADJ_CHUNKS == ADJ_CHUNKS - 1:
+                a = (r - X_ROUNDS) // ADJ_CHUNKS
+                result = work.tile([P, D_OUT], F32, name="result")
+                nc.vector.tensor_scalar_max(out=result[:], in0=sums_of[r][:], scalar1=0.0)
+                nc.sync.dma_start(out=out[a * P : (a + 1) * P, :], in_=result[:])
+
+        def quantise_h(r):
+            cols = slice(r * H_PASSES * D_OUT, (r + 1) * H_PASSES * D_OUT)
+            nc.vector.quantize_mx(
+                out=h_codes[:, cols].bitcast(FP8X4),
+                scales=h_scales[:, cols],
+                in_=h_grouped_of[r][:].rearrange("p g d t -> p (g d t)"),
+            )
+
+        for s in range(ROUNDS + 3):
+            if s >= 3:
+                finish(s - 3)
+            if 1 <= s <= ROUNDS:
+                quantise(s - 1)
+            if 3 <= s < X_ROUNDS + 3:
+                quantise_h(s - 3)
+            if s < ROUNDS:
+                transpose(s)
+            if 2 <= s < ROUNDS + 2:
+                multiply(s - 2)

@@ -6,6 +6,7 @@ BF16 = mybir.dt.bfloat16
 U32 = mybir.dt.uint32
 U8 = mybir.dt.uint8
 FP8X4 = mybir.dt.float8_e4m3fn_x4
+ADD = mybir.AluOpType.add
 
 N_DST, N_SRC, D_IN, D_OUT = 640, 16384, 512, 128
 FLOPS = 2 * N_SRC * D_IN * D_OUT + 2 * N_DST * N_SRC * D_OUT
@@ -20,21 +21,30 @@ BANKS = CHUNK // 2 // BANK_WORDS
 OPERANDS = CHUNK // K_PASS
 
 X_NODES = CHUNK // D_IN * P
-X_ROUNDS = N_SRC // X_NODES
 H_PASSES = OPERANDS // PACK
-ADJ_CHUNKS = N_SRC // CHUNK
-ADJ_ROUNDS = N_DST // P * ADJ_CHUNKS
-ROUNDS = X_ROUNDS + ADJ_ROUNDS
-
-VECTOR_BANKS_X = 0
-VECTOR_BANKS_ADJ = 1
+SPANS = N_SRC // CHUNK
+X_PER_SPAN = CHUNK // X_NODES
+DST_TILES = N_DST // P
+ROUNDS = SPANS * (X_PER_SPAN + DST_TILES)
 
 CHUNK_BUFS = 16
 XPOSE_BANKS = 6
 
 
+def round_order():
+    order = []
+    for j in range(SPANS + 1):
+        for i in range(DST_TILES):
+            if j < SPANS and i < X_PER_SPAN:
+                order.append((True, j * X_PER_SPAN + i, j))
+            if j > 0:
+                order.append((False, i, j - 1))
+    return order
+
+
 def tile_gcn_pa_k_kernel(tc, x, adj, W0, b0, out):
     nc = tc.nc
+    rounds = round_order()
     with (
         tc.tile_pool(name="const", bufs=1) as const,
         tc.tile_pool(name="stream", bufs=CHUNK_BUFS) as stream,
@@ -44,30 +54,33 @@ def tile_gcn_pa_k_kernel(tc, x, adj, W0, b0, out):
         tc.manual_schedule(),
     ):
         chunks = []
-        for r in range(ROUNDS):
+        for is_x, i, span in rounds:
             chunk = stream.tile([P, CHUNK], BF16, name="chunk")
-            if r < X_ROUNDS:
-                nodes = x[r * X_NODES : (r + 1) * X_NODES, :]
+            if is_x:
+                nodes = x[i * X_NODES : (i + 1) * X_NODES, :]
                 nc.sync.dma_start(
                     out=chunk[:].rearrange("p (b w) -> p b w", w=2 * D_IN),
                     in_=nodes.rearrange("(b p e) f -> p b (e f)", p=P, e=2),
                 )
             else:
-                a, c = divmod(r - X_ROUNDS, ADJ_CHUNKS)
                 nc.sync.dma_start(
-                    out=chunk[:], in_=adj[a * P : (a + 1) * P, c * CHUNK : (c + 1) * CHUNK]
+                    out=chunk[:],
+                    in_=adj[i * P : (i + 1) * P, span * CHUNK : (span + 1) * CHUNK],
                 )
             chunks.append(chunk)
+
+        ident = const.tile([P, P], F32, name="ident")
+        make_identity(nc, ident[:])
 
         ones = const.tile([P, P], BF16, name="ones")
         nc.vector.memset(ones[:], 1.0)
         b_rows = const.tile([P, D_OUT], BF16, name="b_rows")
         nc.vector.memset(b_rows[:], 0.0)
         nc.scalar.dma_start(out=b_rows[0:1, :], in_=b0.unsqueeze(0))
-        b_sum = sums.tile([P, D_OUT], F32, name="mx_sum")
-        nc.tensor.matmul(out=b_sum[:], lhsT=ones[:], rhs=b_rows[:], start=True, stop=True)
         bias = const.tile([P, D_OUT], F32, name="bias")
-        nc.vector.tensor_copy(out=bias[:], in_=b_sum[:])
+
+        out_acc = const.tile([P, DST_TILES, D_OUT], F32, name="out_acc")
+        nc.vector.memset(out_acc[:], 0.0)
 
         w_raw = const.tile([P, PACK, D_OUT], BF16, name="w_raw")
         nc.scalar.dma_start(
@@ -84,9 +97,6 @@ def tile_gcn_pa_k_kernel(tc, x, adj, W0, b0, out):
             in_=w_grouped[:].rearrange("p c t -> p (c t)"),
         )
 
-        ident = const.tile([P, P], F32, name="ident")
-        make_identity(nc, ident[:])
-
         h_codes = const.tile([P, N_SRC // K_PASS * D_OUT], U32, name="h_codes", align_bytes=64)
         h_scales = const.tile([P, N_SRC // K_PASS * D_OUT], U8, name="h_scales", align_bytes=64)
 
@@ -96,11 +106,17 @@ def tile_gcn_pa_k_kernel(tc, x, adj, W0, b0, out):
         sums_of = {}
         h_grouped_of = {}
 
+        def spread_bias():
+            b_sum = sums.tile([P, D_OUT], F32, name="mx_sum")
+            nc.tensor.matmul(out=b_sum[:], lhsT=ones[:], rhs=b_rows[:], start=True, stop=True)
+            nc.vector.tensor_copy(out=bias[:], in_=b_sum[:])
+
         def transpose(r):
+            is_x, i, span = rounds[r]
             words = chunks[r][:].bitcast(F32)
             grouped = work.tile([P, CHUNK], BF16, name="grouped", align_bytes=64)
             grouped_words = grouped[:].bitcast(F32)
-            vector_banks = VECTOR_BANKS_X if r < X_ROUNDS else VECTOR_BANKS_ADJ
+            vector_takes_last = not is_x and i % 2 == 1
             for k in range(BANKS):
                 bank = xpose.tile([P, BANK_WORDS], F32, name="bank")
                 for j in range(BLOCKS_PER_BANK):
@@ -112,10 +128,10 @@ def tile_gcn_pa_k_kernel(tc, x, adj, W0, b0, out):
                 dst = grouped_words[:, k * BANK_WORDS : (k + 1) * BANK_WORDS].rearrange(
                     "p (m c u) -> p m c u", u=2, c=P
                 )
-                if k < BANKS - vector_banks:
-                    nc.scalar.copy(out=dst, in_=src)
-                else:
+                if vector_takes_last and k == BANKS - 1:
                     nc.vector.tensor_copy(out=dst, in_=src)
+                else:
+                    nc.scalar.copy(out=dst, in_=src)
             grouped_of[r] = grouped
 
         def quantise(r):
@@ -128,9 +144,10 @@ def tile_gcn_pa_k_kernel(tc, x, adj, W0, b0, out):
             scales_of[r] = scales
 
         def multiply(r):
+            is_x, i, span = rounds[r]
             codes = codes_of[r]
             scales = scales_of[r]
-            if r < X_ROUNDS:
+            if is_x:
                 sums_of[r] = []
                 for g in range(H_PASSES):
                     h_sum = sums.tile([P, PACK, D_OUT], F32, name="mx_sum")
@@ -147,55 +164,61 @@ def tile_gcn_pa_k_kernel(tc, x, adj, W0, b0, out):
                         )
                     sums_of[r].append(h_sum)
             else:
-                c = (r - X_ROUNDS) % ADJ_CHUNKS
-                if c == 0:
-                    out_sum = sums.tile([P, D_OUT], F32, name="mx_sum")
-                else:
-                    out_sum = sums_of[r - 1]
+                out_sum = sums.tile([P, D_OUT], F32, name="mx_sum")
                 for m in range(OPERANDS):
-                    g = c * OPERANDS + m
+                    g = span * OPERANDS + m
                     nc.tensor.matmul_mx(
                         out=out_sum[:],
                         lhsT=codes[:, m * P : (m + 1) * P].bitcast(FP8X4),
                         lhsT_scale=scales[:, m * P : (m + 1) * P],
                         rhs=h_codes[:, g * D_OUT : (g + 1) * D_OUT].bitcast(FP8X4),
                         rhs_scale=h_scales[:, g * D_OUT : (g + 1) * D_OUT],
-                        start=(g == 0),
-                        stop=(g == N_SRC // K_PASS - 1),
+                        start=(m == 0),
+                        stop=(m == OPERANDS - 1),
                     )
                 sums_of[r] = out_sum
 
         def finish(r):
-            if r < X_ROUNDS:
-                h_grouped = work.tile([P, H_PASSES, D_OUT, PACK], BF16, name="h_grouped", align_bytes=64)
+            is_x, i, span = rounds[r]
+            if is_x:
+                h_grouped = work.tile(
+                    [P, H_PASSES, D_OUT, PACK], BF16, name="h_grouped", align_bytes=64
+                )
                 for g, h_sum in enumerate(sums_of[r]):
                     nc.vector.tensor_tensor(
                         out=h_grouped[:, g, :, :],
                         in0=h_sum[:].rearrange("p t d -> p d t"),
                         in1=bias[:].unsqueeze(2).to_broadcast([P, D_OUT, PACK]),
-                        op=mybir.AluOpType.add,
+                        op=ADD,
                     )
                 h_grouped_of[r] = h_grouped
-            elif (r - X_ROUNDS) % ADJ_CHUNKS == ADJ_CHUNKS - 1:
-                a = (r - X_ROUNDS) // ADJ_CHUNKS
-                result = work.tile([P, D_OUT], F32, name="result")
-                nc.vector.tensor_scalar_max(out=result[:], in0=sums_of[r][:], scalar1=0.0)
-                nc.sync.dma_start(out=out[a * P : (a + 1) * P, :], in_=result[:])
+            else:
+                nc.vector.tensor_tensor(
+                    out=out_acc[:, i, :], in0=sums_of[r][:], in1=out_acc[:, i, :], op=ADD
+                )
+                if span == SPANS - 1:
+                    result = work.tile([P, D_OUT], F32, name="result")
+                    nc.vector.tensor_scalar_max(out=result[:], in0=out_acc[:, i, :], scalar1=0.0)
+                    nc.sync.dma_start(out=out[i * P : (i + 1) * P, :], in_=result[:])
 
         def quantise_h(r):
-            cols = slice(r * H_PASSES * D_OUT, (r + 1) * H_PASSES * D_OUT)
-            nc.vector.quantize_mx(
-                out=h_codes[:, cols].bitcast(FP8X4),
-                scales=h_scales[:, cols],
-                in_=h_grouped_of[r][:].rearrange("p g d t -> p (g d t)"),
-            )
+            is_x, i, span = rounds[r]
+            if is_x:
+                cols = slice(i * H_PASSES * D_OUT, (i + 1) * H_PASSES * D_OUT)
+                nc.vector.quantize_mx(
+                    out=h_codes[:, cols].bitcast(FP8X4),
+                    scales=h_scales[:, cols],
+                    in_=h_grouped_of[r][:].rearrange("p g d t -> p (g d t)"),
+                )
 
-        for s in range(ROUNDS + 3):
+        transpose(0)
+        spread_bias()
+        for s in range(1, ROUNDS + 3):
             if s >= 3:
                 finish(s - 3)
-            if 1 <= s <= ROUNDS:
+            if s <= ROUNDS:
                 quantise(s - 1)
-            if 3 <= s < X_ROUNDS + 3:
+            if s >= 3:
                 quantise_h(s - 3)
             if s < ROUNDS:
                 transpose(s)

@@ -18,6 +18,8 @@ CHUNK = 4096
 BANK_WORDS = 512
 BLOCKS_PER_BANK = BANK_WORDS // P
 BANKS = CHUNK // 2 // BANK_WORDS
+BANK_VALUES = 2 * BANK_WORDS
+BANK_PACKED = BANK_VALUES // PACK
 OPERANDS = CHUNK // K_PASS
 
 X_NODES = CHUNK // D_IN * P
@@ -27,8 +29,9 @@ X_PER_SPAN = CHUNK // X_NODES
 DST_TILES = N_DST // P
 ROUNDS = SPANS * (X_PER_SPAN + DST_TILES)
 
-CHUNK_BUFS = 16
-XPOSE_BANKS = 6
+CHUNK_BUFS = 14
+XPOSE_BANKS = 5
+SUM_BANKS = 3
 
 
 def round_order():
@@ -48,9 +51,9 @@ def tile_gcn_pa_k_kernel(tc, x, adj, W0, b0, out):
     with (
         tc.tile_pool(name="const", bufs=1) as const,
         tc.tile_pool(name="stream", bufs=CHUNK_BUFS) as stream,
-        tc.tile_pool(name="work", bufs=3) as work,
+        tc.tile_pool(name="work", bufs=4) as work,
         tc.psum_pool(name="xpose", bufs=XPOSE_BANKS) as xpose,
-        tc.psum_pool(name="sums", bufs=2) as sums,
+        tc.psum_pool(name="sums", bufs=SUM_BANKS) as sums,
         tc.manual_schedule(),
     ):
         chunks = []
@@ -111,7 +114,12 @@ def tile_gcn_pa_k_kernel(tc, x, adj, W0, b0, out):
             nc.tensor.matmul(out=b_sum[:], lhsT=ones[:], rhs=b_rows[:], start=True, stop=True)
             nc.vector.tensor_copy(out=bias[:], in_=b_sum[:])
 
+        def exists(r):
+            return 0 <= r < ROUNDS
+
         def transpose(r):
+            if not exists(r):
+                return
             is_x, i, span = rounds[r]
             words = chunks[r][:].bitcast(F32)
             grouped = work.tile([P, CHUNK], BF16, name="grouped", align_bytes=64)
@@ -135,15 +143,23 @@ def tile_gcn_pa_k_kernel(tc, x, adj, W0, b0, out):
             grouped_of[r] = grouped
 
         def quantise(r):
+            if not exists(r):
+                return
             codes = work.tile([P, OPERANDS * P], U32, name="codes", align_bytes=64)
             scales = work.tile([P, OPERANDS * P], U8, name="scales", align_bytes=64)
-            nc.vector.quantize_mx(
-                out=codes[:].bitcast(FP8X4), scales=scales[:], in_=grouped_of[r][:]
-            )
+            for k in range(BANKS):
+                packed = slice(k * BANK_PACKED, (k + 1) * BANK_PACKED)
+                nc.vector.quantize_mx(
+                    out=codes[:, packed].bitcast(FP8X4),
+                    scales=scales[:, packed],
+                    in_=grouped_of[r][:, k * BANK_VALUES : (k + 1) * BANK_VALUES],
+                )
             codes_of[r] = codes
             scales_of[r] = scales
 
         def multiply(r):
+            if not exists(r):
+                return
             is_x, i, span = rounds[r]
             codes = codes_of[r]
             scales = scales_of[r]
@@ -179,6 +195,8 @@ def tile_gcn_pa_k_kernel(tc, x, adj, W0, b0, out):
                 sums_of[r] = out_sum
 
         def finish(r):
+            if not exists(r):
+                return
             is_x, i, span = rounds[r]
             if is_x:
                 h_grouped = work.tile(
@@ -202,6 +220,8 @@ def tile_gcn_pa_k_kernel(tc, x, adj, W0, b0, out):
                     nc.sync.dma_start(out=out[i * P : (i + 1) * P, :], in_=result[:])
 
         def quantise_h(r):
+            if not exists(r):
+                return
             is_x, i, span = rounds[r]
             if is_x:
                 cols = slice(i * H_PASSES * D_OUT, (i + 1) * H_PASSES * D_OUT)
@@ -211,16 +231,18 @@ def tile_gcn_pa_k_kernel(tc, x, adj, W0, b0, out):
                     in_=h_grouped_of[r][:].rearrange("p g d t -> p (g d t)"),
                 )
 
-        transpose(0)
-        spread_bias()
-        for s in range(1, ROUNDS + 3):
-            if s >= 3:
-                finish(s - 3)
-            if s <= ROUNDS:
-                quantise(s - 1)
-            if s >= 3:
-                quantise_h(s - 3)
-            if s < ROUNDS:
-                transpose(s)
-            if 2 <= s < ROUNDS + 2:
-                multiply(s - 2)
+        for s in range(ROUNDS // 2 + 2):
+            a = 2 * s
+            b = a + 1
+            finish(a - 4)
+            finish(a - 3)
+            quantise(a - 1)
+            quantise_h(a - 4)
+            quantise_h(a - 3)
+            transpose(a)
+            quantise(a)
+            transpose(b)
+            if s == 0:
+                spread_bias()
+            multiply(a - 2)
+            multiply(a - 1)

@@ -56,6 +56,22 @@ def tile_gcn_pa_k_kernel(tc, x, adj, W0, b0, out):
         tc.psum_pool(name="sums", bufs=SUM_BANKS) as sums,
         tc.manual_schedule(),
     ):
+        w_raw = const.tile([P, PACK, D_OUT], BF16, name="w_raw")
+        nc.scalar.dma_start(
+            out=w_raw[:].rearrange("p (u e) c -> p u (e c)", e=2),
+            in_=W0.rearrange("(u p e) c -> p u (e c)", p=P, e=2),
+        )
+
+        ident = const.tile([P, P], F32, name="ident")
+        make_identity(nc, ident[:])
+
+        ones = const.tile([P, P], BF16, name="ones")
+        nc.vector.memset(ones[:], 1.0)
+        b_rows = const.tile([P, D_OUT], BF16, name="b_rows")
+        nc.vector.memset(b_rows[:], 0.0)
+        nc.scalar.dma_start(out=b_rows[0:1, :], in_=b0.unsqueeze(0))
+        bias = const.tile([P, D_OUT], F32, name="bias")
+
         chunks = []
         for is_x, i, span in rounds:
             chunk = stream.tile([P, CHUNK], BF16, name="chunk")
@@ -72,24 +88,9 @@ def tile_gcn_pa_k_kernel(tc, x, adj, W0, b0, out):
                 )
             chunks.append(chunk)
 
-        ident = const.tile([P, P], F32, name="ident")
-        make_identity(nc, ident[:])
-
-        ones = const.tile([P, P], BF16, name="ones")
-        nc.vector.memset(ones[:], 1.0)
-        b_rows = const.tile([P, D_OUT], BF16, name="b_rows")
-        nc.vector.memset(b_rows[:], 0.0)
-        nc.scalar.dma_start(out=b_rows[0:1, :], in_=b0.unsqueeze(0))
-        bias = const.tile([P, D_OUT], F32, name="bias")
-
         out_acc = const.tile([P, DST_TILES, D_OUT], F32, name="out_acc")
         nc.vector.memset(out_acc[:], 0.0)
 
-        w_raw = const.tile([P, PACK, D_OUT], BF16, name="w_raw")
-        nc.scalar.dma_start(
-            out=w_raw[:].rearrange("p (u e) c -> p u (e c)", e=2),
-            in_=W0.rearrange("(u p e) c -> p u (e c)", p=P, e=2),
-        )
         w_grouped = const.tile([P, D_OUT, PACK], BF16, name="w_grouped", align_bytes=64)
         nc.vector.tensor_copy(out=w_grouped[:], in_=w_raw[:].rearrange("p t c -> p c t"))
         w_codes = const.tile([P, D_OUT], U32, name="w_codes", align_bytes=64)

@@ -18,8 +18,7 @@ CHUNK = 4096
 BANK_WORDS = 512
 BLOCKS_PER_BANK = BANK_WORDS // P
 BANKS = CHUNK // 2 // BANK_WORDS
-BANK_VALUES = 2 * BANK_WORDS
-BANK_PACKED = BANK_VALUES // PACK
+X_HALF_WORDS = CHUNK // 4
 OPERANDS = CHUNK // K_PASS
 
 X_NODES = CHUNK // D_IN * P
@@ -78,8 +77,7 @@ def tile_gcn_pa_k_kernel(tc, x, adj, W0, b0, out):
             if is_x:
                 nodes = x[i * X_NODES : (i + 1) * X_NODES, :]
                 nc.sync.dma_start(
-                    out=chunk[:].rearrange("p (b w) -> p b w", w=2 * D_IN),
-                    in_=nodes.rearrange("(b p e) f -> p b (e f)", p=P, e=2),
+                    out=chunk[:], in_=nodes.rearrange("(p j) f -> p (j f)", p=P)
                 )
             else:
                 nc.sync.dma_start(
@@ -128,15 +126,24 @@ def tile_gcn_pa_k_kernel(tc, x, adj, W0, b0, out):
             vector_takes_last = not is_x and i % 2 == 1
             for k in range(BANKS):
                 bank = xpose.tile([P, BANK_WORDS], F32, name="bank")
-                for j in range(BLOCKS_PER_BANK):
-                    block = k * BLOCKS_PER_BANK + j
+                if is_x:
+                    e, q = divmod(k, 2)
+                    blocks = [2 * (4 * q + 2 * n + e) + u for n in range(2) for u in range(2)]
+                else:
+                    blocks = range(k * BLOCKS_PER_BANK, (k + 1) * BLOCKS_PER_BANK)
+                for j, block in enumerate(blocks):
                     nc.tensor.transpose(
                         bank[:, j * P : (j + 1) * P], words[:, block * P : (block + 1) * P], ident[:]
                     )
-                src = bank[:].rearrange("p (m u c) -> p m c u", u=2, c=P)
-                dst = grouped_words[:, k * BANK_WORDS : (k + 1) * BANK_WORDS].rearrange(
-                    "p (m c u) -> p m c u", u=2, c=P
-                )
+                if is_x:
+                    src = bank[:].rearrange("p (v s) -> p s v", s=P)
+                    half = grouped_words[:, e * X_HALF_WORDS : (e + 1) * X_HALF_WORDS]
+                    dst = half.rearrange("p (s q v) -> p q s v", s=P, q=2)[:, q, :, :]
+                else:
+                    src = bank[:].rearrange("p (m u c) -> p m c u", u=2, c=P)
+                    dst = grouped_words[:, k * BANK_WORDS : (k + 1) * BANK_WORDS].rearrange(
+                        "p (m c u) -> p m c u", u=2, c=P
+                    )
                 if vector_takes_last and k == BANKS - 1:
                     nc.vector.tensor_copy(out=dst, in_=src)
                 else:
@@ -148,12 +155,14 @@ def tile_gcn_pa_k_kernel(tc, x, adj, W0, b0, out):
                 return
             codes = work.tile([P, OPERANDS * P], U32, name="codes", align_bytes=64)
             scales = work.tile([P, OPERANDS * P], U8, name="scales", align_bytes=64)
-            for k in range(BANKS):
-                packed = slice(k * BANK_PACKED, (k + 1) * BANK_PACKED)
+            calls = 2 if rounds[r][0] else BANKS
+            width = OPERANDS * P // calls
+            for k in range(calls):
+                packed = slice(k * width, (k + 1) * width)
                 nc.vector.quantize_mx(
                     out=codes[:, packed].bitcast(FP8X4),
                     scales=scales[:, packed],
-                    in_=grouped_of[r][:, k * BANK_VALUES : (k + 1) * BANK_VALUES],
+                    in_=grouped_of[r][:, k * width * PACK : (k + 1) * width * PACK],
                 )
             codes_of[r] = codes
             scales_of[r] = scales
@@ -169,7 +178,8 @@ def tile_gcn_pa_k_kernel(tc, x, adj, W0, b0, out):
                 for g in range(H_PASSES):
                     h_sum = sums.tile([P, PACK, D_OUT], F32, name="mx_sum")
                     for t in range(PACK):
-                        cols = slice((g * PACK + t) * P, (g * PACK + t + 1) * P)
+                        m = 4 * (t % 2) + 2 * g + t // 2
+                        cols = slice(m * P, (m + 1) * P)
                         nc.tensor.matmul_mx(
                             out=h_sum[:, t, :],
                             lhsT=codes[:, cols].bitcast(FP8X4),

@@ -242,18 +242,11 @@ def tile_gcn_pa_k_kernel(tc, x, adj, W0, b0, out):
                     in_=h_grouped_of[r][:].rearrange("p g d t -> p (g d t)"),
                 )
 
-        for s in range(ROUNDS // 2 + 2):
-            a = 2 * s
-            b = a + 1
-            finish(a - 4)
-            finish(a - 3)
-            quantise(a - 1)
-            quantise_h(a - 4)
-            quantise_h(a - 3)
-            transpose(a)
-            quantise(a)
-            transpose(b)
-            if s == 0:
+        for r in range(ROUNDS + 3):
+            finish(r - 3)
+            quantise(r - 1)
+            quantise_h(r - 3)
+            transpose(r)
+            if r == 1:
                 spread_bias()
-            multiply(a - 2)
-            multiply(a - 1)
+            multiply(r - 2)

import concourse.mybir as mybir
from concourse.masks import make_identity

F32 = mybir.dt.float32
BF16 = mybir.dt.bfloat16
U32 = mybir.dt.uint32
U8 = mybir.dt.uint8
FP8X4 = mybir.dt.float8_e4m3fn_x4
ADD = mybir.AluOpType.add

N_DST, N_SRC, D_IN, D_OUT = 640, 16384, 512, 128
FLOPS = 2 * N_SRC * D_IN * D_OUT + 2 * N_DST * N_SRC * D_OUT

P = 128
PACK = 4
K_PASS = P * PACK
CHUNK = 4096
BANK_WORDS = 512
BLOCKS_PER_BANK = BANK_WORDS // P
BANKS = CHUNK // 2 // BANK_WORDS
X_HALF_WORDS = CHUNK // 4
OPERANDS = CHUNK // K_PASS

X_NODES = CHUNK // D_IN * P
H_PASSES = OPERANDS // PACK
SPANS = N_SRC // CHUNK
X_PER_SPAN = CHUNK // X_NODES
DST_TILES = N_DST // P
ROUNDS = SPANS * (X_PER_SPAN + DST_TILES)

CHUNK_BUFS = 14
XPOSE_BANKS = 5
SUM_BANKS = 3


def round_order():
    order = []
    for j in range(SPANS + 1):
        for i in range(DST_TILES):
            if j < SPANS and i < X_PER_SPAN:
                order.append((True, j * X_PER_SPAN + i, j))
            if j > 0:
                order.append((False, i, j - 1))
    return order


def tile_gcn_pa_k_kernel(tc, x, adj, W0, b0, out):
    nc = tc.nc
    rounds = round_order()
    with (
        tc.tile_pool(name="const", bufs=1) as const,
        tc.tile_pool(name="stream", bufs=CHUNK_BUFS) as stream,
        tc.tile_pool(name="work", bufs=4) as work,
        tc.psum_pool(name="xpose", bufs=XPOSE_BANKS) as xpose,
        tc.psum_pool(name="sums", bufs=SUM_BANKS) as sums,
        tc.manual_schedule(),
    ):
        w_raw = const.tile([P, PACK, D_OUT], BF16, name="w_raw")
        nc.scalar.dma_start(
            out=w_raw[:].rearrange("p (u e) c -> p u (e c)", e=2),
            in_=W0.rearrange("(u p e) c -> p u (e c)", p=P, e=2),
        )

        ident = const.tile([P, P], F32, name="ident")
        make_identity(nc, ident[:])

        ones = const.tile([P, P], BF16, name="ones")
        nc.vector.memset(ones[:], 1.0)
        b_rows = const.tile([P, D_OUT], BF16, name="b_rows")
        nc.vector.memset(b_rows[:], 0.0)
        nc.scalar.dma_start(out=b_rows[0:1, :], in_=b0.unsqueeze(0))
        bias = const.tile([P, D_OUT], F32, name="bias")

        chunks = []
        for is_x, i, span in rounds:
            chunk = stream.tile([P, CHUNK], BF16, name="chunk")
            if is_x:
                nodes = x[i * X_NODES : (i + 1) * X_NODES, :]
                nc.sync.dma_start(
                    out=chunk[:], in_=nodes.rearrange("(p j) f -> p (j f)", p=P)
                )
            else:
                nc.sync.dma_start(
                    out=chunk[:],
                    in_=adj[i * P : (i + 1) * P, span * CHUNK : (span + 1) * CHUNK],
                )
            chunks.append(chunk)

        out_acc = const.tile([P, DST_TILES, D_OUT], F32, name="out_acc")
        nc.vector.memset(out_acc[:], 0.0)

        w_grouped = const.tile([P, D_OUT, PACK], BF16, name="w_grouped", align_bytes=64)
        nc.vector.tensor_copy(out=w_grouped[:], in_=w_raw[:].rearrange("p t c -> p c t"))
        w_codes = const.tile([P, D_OUT], U32, name="w_codes", align_bytes=64)
        w_scales = const.tile([P, D_OUT], U8, name="w_scales", align_bytes=64)
        nc.vector.quantize_mx(
            out=w_codes[:].bitcast(FP8X4),
            scales=w_scales[:],
            in_=w_grouped[:].rearrange("p c t -> p (c t)"),
        )

        h_codes = const.tile([P, N_SRC // K_PASS * D_OUT], U32, name="h_codes", align_bytes=64)
        h_scales = const.tile([P, N_SRC // K_PASS * D_OUT], U8, name="h_scales", align_bytes=64)

        grouped_of = {}
        codes_of = {}
        scales_of = {}
        sums_of = {}
        h_grouped_of = {}

        def spread_bias():
            b_sum = sums.tile([P, D_OUT], F32, name="mx_sum")
            nc.tensor.matmul(out=b_sum[:], lhsT=ones[:], rhs=b_rows[:], start=True, stop=True)
            nc.vector.tensor_copy(out=bias[:], in_=b_sum[:])

        def exists(r):
            return 0 <= r < ROUNDS

        def transpose(r):
            if not exists(r):
                return
            is_x, i, span = rounds[r]
            words = chunks[r][:].bitcast(F32)
            grouped = work.tile([P, CHUNK], BF16, name="grouped", align_bytes=64)
            grouped_words = grouped[:].bitcast(F32)
            vector_takes_last = not is_x and i % 2 == 1
            for k in range(BANKS):
                bank = xpose.tile([P, BANK_WORDS], F32, name="bank")
                if is_x:
                    e, q = divmod(k, 2)
                    blocks = [2 * (4 * q + 2 * n + e) + u for n in range(2) for u in range(2)]
                else:
                    blocks = range(k * BLOCKS_PER_BANK, (k + 1) * BLOCKS_PER_BANK)
                for j, block in enumerate(blocks):
                    nc.tensor.transpose(
                        bank[:, j * P : (j + 1) * P], words[:, block * P : (block + 1) * P], ident[:]
                    )
                if is_x:
                    src = bank[:].rearrange("p (v s) -> p s v", s=P)
                    half = grouped_words[:, e * X_HALF_WORDS : (e + 1) * X_HALF_WORDS]
                    dst = half.rearrange("p (s q v) -> p q s v", s=P, q=2)[:, q, :, :]
                else:
                    src = bank[:].rearrange("p (m u c) -> p m c u", u=2, c=P)
                    dst = grouped_words[:, k * BANK_WORDS : (k + 1) * BANK_WORDS].rearrange(
                        "p (m c u) -> p m c u", u=2, c=P
                    )
                if vector_takes_last and k == BANKS - 1:
                    nc.vector.tensor_copy(out=dst, in_=src)
                else:
                    nc.scalar.copy(out=dst, in_=src)
            grouped_of[r] = grouped

        def quantise(r):
            if not exists(r):
                return
            codes = work.tile([P, OPERANDS * P], U32, name="codes", align_bytes=64)
            scales = work.tile([P, OPERANDS * P], U8, name="scales", align_bytes=64)
            calls = 2 if rounds[r][0] else BANKS
            width = OPERANDS * P // calls
            for k in range(calls):
                packed = slice(k * width, (k + 1) * width)
                nc.vector.quantize_mx(
                    out=codes[:, packed].bitcast(FP8X4),
                    scales=scales[:, packed],
                    in_=grouped_of[r][:, k * width * PACK : (k + 1) * width * PACK],
                )
            codes_of[r] = codes
            scales_of[r] = scales

        def multiply(r):
            if not exists(r):
                return
            is_x, i, span = rounds[r]
            codes = codes_of[r]
            scales = scales_of[r]
            if is_x:
                sums_of[r] = []
                for g in range(H_PASSES):
                    h_sum = sums.tile([P, PACK, D_OUT], F32, name="mx_sum")
                    for t in range(PACK):
                        m = 4 * (t % 2) + 2 * g + t // 2
                        cols = slice(m * P, (m + 1) * P)
                        nc.tensor.matmul_mx(
                            out=h_sum[:, t, :],
                            lhsT=codes[:, cols].bitcast(FP8X4),
                            lhsT_scale=scales[:, cols],
                            rhs=w_codes[:].bitcast(FP8X4),
                            rhs_scale=w_scales[:],
                            start=True,
                            stop=True,
                        )
                    sums_of[r].append(h_sum)
            else:
                out_sum = sums.tile([P, D_OUT], F32, name="mx_sum")
                for m in range(OPERANDS):
                    g = span * OPERANDS + m
                    nc.tensor.matmul_mx(
                        out=out_sum[:],
                        lhsT=codes[:, m * P : (m + 1) * P].bitcast(FP8X4),
                        lhsT_scale=scales[:, m * P : (m + 1) * P],
                        rhs=h_codes[:, g * D_OUT : (g + 1) * D_OUT].bitcast(FP8X4),
                        rhs_scale=h_scales[:, g * D_OUT : (g + 1) * D_OUT],
                        start=(m == 0),
                        stop=(m == OPERANDS - 1),
                    )
                sums_of[r] = out_sum

        def finish(r):
            if not exists(r):
                return
            is_x, i, span = rounds[r]
            if is_x:
                h_grouped = work.tile(
                    [P, H_PASSES, D_OUT, PACK], BF16, name="h_grouped", align_bytes=64
                )
                for g, h_sum in enumerate(sums_of[r]):
                    nc.vector.tensor_tensor(
                        out=h_grouped[:, g, :, :],
                        in0=h_sum[:].rearrange("p t d -> p d t"),
                        in1=bias[:].unsqueeze(2).to_broadcast([P, D_OUT, PACK]),
                        op=ADD,
                    )
                h_grouped_of[r] = h_grouped
            else:
                nc.vector.tensor_tensor(
                    out=out_acc[:, i, :], in0=sums_of[r][:], in1=out_acc[:, i, :], op=ADD
                )
                if span == SPANS - 1:
                    result = work.tile([P, D_OUT], F32, name="result")
                    nc.vector.tensor_scalar_max(out=result[:], in0=out_acc[:, i, :], scalar1=0.0)
                    nc.sync.dma_start(out=out[i * P : (i + 1) * P, :], in_=result[:])

        def quantise_h(r):
            if not exists(r):
                return
            is_x, i, span = rounds[r]
            if is_x:
                cols = slice(i * H_PASSES * D_OUT, (i + 1) * H_PASSES * D_OUT)
                nc.vector.quantize_mx(
                    out=h_codes[:, cols].bitcast(FP8X4),
                    scales=h_scales[:, cols],
                    in_=h_grouped_of[r][:].rearrange("p g d t -> p (g d t)"),
                )

        for r in range(ROUNDS + 3):
            finish(r - 3)
            quantise(r - 1)
            quantise_h(r - 3)
            transpose(r)
            if r == 1:
                spread_bias()
            multiply(r - 2)
